import numpy as np
import ml_dtypes


def mxq(x, axis, fmt="e4m3"):
    dtype, down = {"e4m3": (ml_dtypes.float8_e4m3fn, 7), "e5m2": (ml_dtypes.float8_e5m2, 14)}[fmt]
    v = np.moveaxis(np.asarray(x, np.float32).astype(ml_dtypes.bfloat16).astype(np.float64), axis, -1)
    blocks = v.reshape(v.shape[:-1] + (-1, 32))
    amax = np.abs(blocks).max(-1, keepdims=True)
    byte = np.maximum(np.where(amax > 0, np.frexp(amax)[1] - 1 + 127, 0) - down, 1)
    scale = np.exp2(byte - 127.0)
    codes = (blocks / scale).astype(np.float32).astype(dtype).astype(np.float64)
    return np.moveaxis((codes * scale).reshape(v.shape), -1, axis)


WIDE = False


def mx_kscale(k):
    if not WIDE:
        return np.ones(k)
    levels = np.array([10, -10, 5, -5, 0])
    if k % 512:
        return np.exp2(np.random.permutation(np.resize(levels, k // 32))).repeat(32)
    a = np.empty((k // 512, 16))
    for p in range(k // 512):
        a[p, :8] = np.random.permutation(np.resize(levels, 8))
        for g in range(8):
            far = levels[np.abs(levels - a[p, g]) >= 10]
            a[p, g + 8] = far[np.random.randint(len(far))]
    return np.exp2(a.ravel()).repeat(32)


BF16 = ml_dtypes.bfloat16


def bf(x):
    return np.asarray(x, np.float32).astype(BF16)


def f64(x):
    return np.asarray(x).astype(np.float64)


T, S, B, E, Z = 512, 512, 2, 1024, 128
N = T * B


def sigmoid(v):
    return 1.0 / (1.0 + np.exp(-v))


def setup_inputs():
    s = mx_kscale(N).reshape(T, B, 1)
    v = mx_kscale(E)
    query = bf(np.random.standard_normal((T, B, E)))
    hr0 = bf(np.random.standard_normal((T, B, E)) * 0.2)
    Wu = bf(np.random.standard_normal((E, E)) / np.sqrt(E))
    bu = bf(np.random.standard_normal(E) * 0.3)
    Wh0 = bf(np.random.standard_normal((E, E)) * 5.0 / np.sqrt(E))
    bh = bf(np.random.standard_normal(E) * 0.3)
    g = bf(np.random.standard_normal((T, B, E)) * np.exp2(np.random.randint(-6, 1, (T, B, 1))) * 4.0 / s * v)
    u = sigmoid(f64(query) @ f64(Wu).T + f64(bu))
    h = np.tanh(f64(hr0) @ f64(Wh0).T + f64(bh))
    return {"query": query, "hr": bf(f64(hr0) * s), "Wu": Wu, "bu": bu,
            "Wh": bf(f64(Wh0) / v[:, None]), "bh": bh,
            "u": np.asarray(u, np.float32), "h": np.asarray(h, np.float32), "grad_out": g}


def reference(query, hr, Wu, bu, Wh, bh, u, h, grad_out):
    hf = f64(h)
    dz = f64(grad_out) * f64(u) * (1.0 - hf * hf)
    dz2 = dz.reshape(N, E)
    a = f64(hr).reshape(N, E)
    dhr = mxq(dz2, 1, "e5m2") @ mxq(f64(Wh), 0, "e4m3")
    dWh = mxq(dz2, 0, "e5m2").T @ mxq(a, 0, "e4m3")
    return dhr.reshape(T, B, E), dWh

@@ -1,0 +1,272 @@
+from contextlib import ExitStack
+
+import concourse.mybir as mybir
+from concourse.masks import make_identity
+
+F32 = mybir.dt.float32
+BF16 = mybir.dt.bfloat16
+U32 = mybir.dt.uint32
+U8 = mybir.dt.uint8
+E4 = mybir.dt.float8_e4m3fn_x4
+E5 = mybir.dt.float8_e5m2_x4
+ALU = mybir.AluOpType
+ACT = mybir.ActivationFunctionType
+
+P = 128
+E = 1024
+G = 2
+J = 4
+NH = 512
+
+FLOPS = 2 * 2 * 1024 * 1024 * 1024
+BYTES = 22 * 1024 * 1024
+
+
+def tile_gatedcrossattention_pb_v_kernel(tc, query, hr, Wu, bu, Wh, bh, u, h, grad_out, out_0, out_1):
+    nc = tc.nc
+    gv = grad_out.flatten_outer_dims().rearrange("(g p j) e -> p g j e", g=G, j=J)
+    uv = u.flatten_outer_dims().rearrange("(g p j) e -> p g j e", g=G, j=J)
+    hv = h.flatten_outer_dims().rearrange("(g p j) e -> p g j e", g=G, j=J)
+    rv = hr.flatten_outer_dims().rearrange("(g p j) e -> p g j e", g=G, j=J)
+    wv = Wh.rearrange("(g p j) e -> p g j e", g=G, j=J)
+    o0v = out_0.flatten_outer_dims().rearrange("(g p j) e -> p g j e", g=G, j=J)
+    o1v = out_1.rearrange("(f p) e -> p f e", p=P)
+
+    with ExitStack() as ctx:
+        const = ctx.enter_context(tc.tile_pool(name="const", bufs=1))
+        raw = ctx.enter_context(tc.tile_pool(name="raw", bufs=1))
+        keep = ctx.enter_context(tc.tile_pool(name="keep", bufs=1))
+        stage = ctx.enter_context(tc.tile_pool(name="stage", bufs=5))
+        tstage = ctx.enter_context(tc.tile_pool(name="tstage", bufs=3))
+        ostage = ctx.enter_context(tc.tile_pool(name="ostage", bufs=7))
+        tpsum = ctx.enter_context(tc.psum_pool(name="tpsum", bufs=2))
+        apsum = ctx.enter_context(tc.psum_pool(name="apsum", bufs=6))
+        ctx.enter_context(tc.manual_schedule())
+
+        ident = const.tile([P, P], F32, name="ident")
+        make_identity(nc, ident[:])
+        ident_bf = const.tile([P, P], BF16, name="ident_bf")
+        make_identity(nc, ident_bf[:])
+        warm = const.tile([P, 1], F32, name="warm")
+        nc.vector.memset(warm[:], 0.0)
+        nc.scalar.activation(out=warm[:], in_=warm[:], func=ACT.Square)
+
+        src = {}
+        rows = {}
+
+        def load_tokens(g, j):
+            gt = raw.tile([P, E], BF16, name="g%d%d" % (g, j))
+            ut = raw.tile([P, E], F32, name="u%d%d" % (g, j))
+            ht = raw.tile([P, E], F32, name="h%d%d" % (g, j))
+            nc.sync.dma_start(out=gt[:], in_=gv[:, g, j, :])
+            nc.sync.dma_start(out=ut[:], in_=uv[:, g, j, :])
+            nc.sync.dma_start(out=ht[:], in_=hv[:, g, j, :])
+            src[(g, j)] = (gt, ut, ht)
+
+        def load_rows(nm, view, g):
+            t = raw.tile([P, J, E], BF16, name="%s%d" % (nm, g))
+            nc.sync.dma_start(out=t[:], in_=view[:, g, :, :])
+            rows[(nm, g)] = t
+
+        load_rows("w", wv, 0)
+        load_rows("w", wv, 1)
+        for j in range(J):
+            load_tokens(0, j)
+        load_rows("r", rv, 0)
+        load_rows("r", rv, 1)
+        for j in range(J):
+            load_tokens(1, j)
+
+        for g in range(G):
+            rows[("d", g)] = keep.tile([P, J, E], BF16, name="dz%d" % g)
+        codes = {}
+        scales = {}
+        for nm in ("w", "r", "d"):
+            codes[nm] = keep.tile([P, G, E], U32, name="%s_codes" % nm, align_bytes=64)
+            scales[nm] = keep.tile([P, G, E], U8, name="%s_scales" % nm, align_bytes=64)
+        fmt = {"w": E4, "r": E4, "d": E5}
+        t_codes = keep.tile([P, G * J, G, P], U32, name="t_codes", align_bytes=64)
+        t_scales = keep.tile([P, G * J, G, P], U8, name="t_scales", align_bytes=64)
+
+        live = {}
+
+        def square(g, j):
+            hs = src[(g, j)][2]
+            nc.scalar.activation(out=hs[:], in_=hs[:], func=ACT.Square)
+
+        def gate(g, j):
+            gs, us, hs = src[(g, j)]
+            nc.vector.scalar_tensor_tensor(out=us[:], in0=gs[:], scalar=-1.0, in1=us[:], op0=ALU.mult, op1=ALU.mult)
+
+        def dz(g, j):
+            gs, us, hs = src[(g, j)]
+            nc.vector.scalar_tensor_tensor(out=rows[("d", g)][:, j, :], in0=hs[:], scalar=1.0, in1=us[:], op0=ALU.subtract, op1=ALU.mult)
+
+        def turn(g, j):
+            words = rows[("d", g)][:, j, :].bitcast(F32)
+            tp = tpsum.tile([P, 4 * P], F32, name="tp")
+            for c in range(G):
+                for w in range(2):
+                    nc.tensor.transpose(tp[:, (2 * c + w) * P:(2 * c + w + 1) * P], words[:, 256 * c + w:256 * (c + 1):2], ident[:])
+            live[("tp", g, j)] = tp
+
+        def turn_out(g, j):
+            tp = live.pop(("tp", g, j))
+            grouped = tstage.tile([P, 4 * 2 * P], BF16, name="grouped", align_bytes=64)
+            nc.scalar.copy(
+                out=grouped[:].bitcast(F32).rearrange("p (c m w) -> p c m w", c=G, w=2),
+                in_=tp[:].rearrange("p (c w m) -> p c m w", c=G, w=2),
+            )
+            live[("gr", g, j)] = grouped
+
+        def turn_quant(g, j):
+            k = g * J + j
+            grouped = live.pop(("gr", g, j))
+            nc.vector.quantize_mx(
+                out=t_codes[:, k, :, :].rearrange("p c m -> p (c m)").bitcast(E5),
+                scales=t_scales[:, k, :, :].rearrange("p c m -> p (c m)"),
+                in_=grouped[:],
+            )
+
+        def weave(nm, g, n, eng):
+            inter = stage.tile([P, NH * J], BF16, name="inter", align_bytes=64)
+            view = rows[(nm, g)][:, :, n * NH:(n + 1) * NH].rearrange("p j w -> p w j")
+            dst = inter[:].rearrange("p (w j) -> p w j", j=J)
+            if eng == "s":
+                nc.scalar.copy(out=dst, in_=view)
+            else:
+                nc.vector.tensor_copy(out=dst, in_=view)
+            live[("in", nm, g, n)] = inter
+
+        def weave_pe(nm, g, n):
+            for b in range(2):
+                bank = apsum.tile([P, NH], F32, name="acc")
+                half = bank[:].bitcast(BF16)
+                for i in range(2):
+                    c0 = n * NH + (2 * b + i) * P
+                    nc.tensor.matmul(
+                        out=half[:, i * NH:(i + 1) * NH].rearrange("p (w j) -> p w j", j=J),
+                        lhsT=ident_bf[:],
+                        rhs=rows[(nm, g)][:, :, c0:c0 + P].rearrange("p j w -> p w j"),
+                        start=True,
+                        stop=True,
+                    )
+                live[("ip", nm, g, n, b)] = bank
+
+        def weave_out(nm, g, n):
+            inter = stage.tile([P, NH * J], BF16, name="inter", align_bytes=64)
+            for b in range(2):
+                bank = live.pop(("ip", nm, g, n, b))
+                nc.scalar.copy(out=inter[:, b * 2 * NH:(b + 1) * 2 * NH], in_=bank[:].bitcast(BF16))
+            live[("in", nm, g, n)] = inter
+
+        def quant(nm, g, n):
+            inter = live.pop(("in", nm, g, n))
+            nc.vector.quantize_mx(
+                out=codes[nm][:, g, n * NH:(n + 1) * NH].bitcast(fmt[nm]),
+                scales=scales[nm][:, g, n * NH:(n + 1) * NH],
+                in_=inter[:],
+            )
+
+        def mult(key, lc, ls, rn):
+            for n in range(2):
+                acc = apsum.tile([P, NH], F32, name="acc")
+                for c in range(G):
+                    nc.tensor.matmul_mx(
+                        out=acc[:],
+                        lhsT=lc[c].bitcast(E5),
+                        lhsT_scale=ls[c],
+                        rhs=codes[rn][:, c, n * NH:(n + 1) * NH].bitcast(E4),
+                        rhs_scale=scales[rn][:, c, n * NH:(n + 1) * NH],
+                        start=(c == 0),
+                        stop=(c == G - 1),
+                    )
+                live[("acc", key, n)] = acc
+
+        def empty(key, dest, engs):
+            o = ostage.tile([P, E], F32, name="o")
+            for n in range(2):
+                acc = live.pop(("acc", key, n))
+                if engs[n] == "s":
+                    nc.scalar.copy(out=o[:, n * NH:(n + 1) * NH], in_=acc[:])
+                else:
+                    nc.vector.tensor_copy(out=o[:, n * NH:(n + 1) * NH], in_=acc[:])
+            nc.sync.dma_start(out=dest, in_=o[:])
+
+        def out0_mult(k):
+            mult(("a", k), [t_codes[:, k, c, :] for c in range(G)], [t_scales[:, k, c, :] for c in range(G)], "w")
+
+        def out0_empty(k, engs):
+            empty(("a", k), o0v[:, k // J, k % J, :], engs)
+
+        def out1_mult(f):
+            mult(("b", f), [codes["d"][:, c, f * P:(f + 1) * P] for c in range(G)],
+                 [scales["d"][:, c, f * P:(f + 1) * P] for c in range(G)], "r")
+
+        def out1_empty(f, engs):
+            empty(("b", f), o1v[:, f, :], engs)
+
+        def step(k, look_ahead):
+            g, j = k // J, k % J
+            dz(g, j)
+            turn(g, j)
+            if j >= 1:
+                turn_quant(g, j - 1)
+            if look_ahead:
+                square((k + 1) // J, (k + 1) % J)
+                gate((k + 1) // J, (k + 1) % J)
+            turn_out(g, j)
+            if j >= 1:
+                out0_mult(k - 1)
+                out0_empty(k - 1, "ss")
+
+        weave_pe("w", 0, 0)
+        weave_pe("w", 0, 1)
+        weave_pe("w", 1, 0)
+        weave_out("w", 0, 0)
+        weave_pe("w", 1, 1)
+        weave_out("w", 0, 1)
+        quant("w", 0, 0)
+        weave_out("w", 1, 0)
+        quant("w", 0, 1)
+        weave_out("w", 1, 1)
+        square(0, 0)
+        gate(0, 0)
+        quant("w", 1, 0)
+        quant("w", 1, 1)
+        for k in range(4):
+            step(k, k < 3)
+        weave("d", 0, 0, "v")
+        turn_quant(0, 3)
+        weave_pe("r", 0, 0)
+        weave_pe("r", 0, 1)
+        out0_mult(3)
+        weave("d", 0, 1, "v")
+        quant("d", 0, 0)
+        weave_out("r", 0, 0)
+        weave_out("r", 0, 1)
+        out0_empty(3, "ss")
+        weave("r", 1, 0, "v")
+        quant("d", 0, 1)
+        quant("r", 0, 0)
+        quant("r", 0, 1)
+        square(1, 0)
+        gate(1, 0)
+        quant("r", 1, 0)
+        weave("r", 1, 1, "s")
+        for k in range(4, 8):
+            step(k, k < 7)
+            if k == 4:
+                quant("r", 1, 1)
+        weave("d", 1, 0, "v")
+        weave("d", 1, 1, "v")
+        turn_quant(1, 3)
+        quant("d", 1, 0)
+        out0_mult(7)
+        quant("d", 1, 1)
+        out1_mult(0)
+        out0_empty(7, "sv")
+        for f in range(1, 8):
+            out1_mult(f)
+            out1_empty(f - 1, "sv")
+        out1_empty(7, "sv")

@@ -36,7 +36,7 @@ def tile_gatedcrossattention_pb_v_kernel(tc, query, hr, Wu, bu, Wh, bh, u, h, gr
         const = ctx.enter_context(tc.tile_pool(name="const", bufs=1))
         raw = ctx.enter_context(tc.tile_pool(name="raw", bufs=1))
         keep = ctx.enter_context(tc.tile_pool(name="keep", bufs=1))
-        stage = ctx.enter_context(tc.tile_pool(name="stage", bufs=5))
+        stage = ctx.enter_context(tc.tile_pool(name="stage", bufs=6))
         tstage = ctx.enter_context(tc.tile_pool(name="tstage", bufs=3))
         ostage = ctx.enter_context(tc.tile_pool(name="ostage", bufs=7))
         tpsum = ctx.enter_context(tc.psum_pool(name="tpsum", bufs=2))
@@ -45,8 +45,6 @@ def tile_gatedcrossattention_pb_v_kernel(tc, query, hr, Wu, bu, Wh, bh, u, h, gr
 
         ident = const.tile([P, P], F32, name="ident")
         make_identity(nc, ident[:])
-        ident_bf = const.tile([P, P], BF16, name="ident_bf")
-        make_identity(nc, ident_bf[:])
         warm = const.tile([P, 1], F32, name="warm")
         nc.vector.memset(warm[:], 0.0)
         nc.scalar.activation(out=warm[:], in_=warm[:], func=ACT.Square)
@@ -70,12 +68,11 @@ def tile_gatedcrossattention_pb_v_kernel(tc, query, hr, Wu, bu, Wh, bh, u, h, gr
 
         load_rows("w", wv, 0)
         load_rows("w", wv, 1)
-        for j in range(J):
-            load_tokens(0, j)
         load_rows("r", rv, 0)
         load_rows("r", rv, 1)
-        for j in range(J):
-            load_tokens(1, j)
+        for g in range(G):
+            for j in range(J):
+                load_tokens(g, j)
 
         for g in range(G):
             rows[("d", g)] = keep.tile([P, J, E], BF16, name="dz%d" % g)
@@ -138,28 +135,6 @@ def tile_gatedcrossattention_pb_v_kernel(tc, query, hr, Wu, bu, Wh, bh, u, h, gr
                 nc.vector.tensor_copy(out=dst, in_=view)
             live[("in", nm, g, n)] = inter
 
-        def weave_pe(nm, g, n):
-            for b in range(2):
-                bank = apsum.tile([P, NH], F32, name="acc")
-                half = bank[:].bitcast(BF16)
-                for i in range(2):
-                    c0 = n * NH + (2 * b + i) * P
-                    nc.tensor.matmul(
-                        out=half[:, i * NH:(i + 1) * NH].rearrange("p (w j) -> p w j", j=J),
-                        lhsT=ident_bf[:],
-                        rhs=rows[(nm, g)][:, :, c0:c0 + P].rearrange("p j w -> p w j"),
-                        start=True,
-                        stop=True,
-                    )
-                live[("ip", nm, g, n, b)] = bank
-
-        def weave_out(nm, g, n):
-            inter = stage.tile([P, NH * J], BF16, name="inter", align_bytes=64)
-            for b in range(2):
-                bank = live.pop(("ip", nm, g, n, b))
-                nc.scalar.copy(out=inter[:, b * 2 * NH:(b + 1) * 2 * NH], in_=bank[:].bitcast(BF16))
-            live[("in", nm, g, n)] = inter
-
         def quant(nm, g, n):
             inter = live.pop(("in", nm, g, n))
             nc.vector.quantize_mx(
@@ -206,67 +181,64 @@ def tile_gatedcrossattention_pb_v_kernel(tc, query, hr, Wu, bu, Wh, bh, u, h, gr
         def out1_empty(f, engs):
             empty(("b", f), o1v[:, f, :], engs)
 
-        def step(k, look_ahead):
+        def step(k):
             g, j = k // J, k % J
             dz(g, j)
             turn(g, j)
-            if j >= 1:
-                turn_quant(g, j - 1)
-            if look_ahead:
+            if k < 7:
                 square((k + 1) // J, (k + 1) % J)
                 gate((k + 1) // J, (k + 1) % J)
+            if 1 <= k < 7:
+                turn_quant((k - 1) // J, (k - 1) % J)
+            if k == 0:
+                quant("r", 1, 1)
+            if k == 4:
+                weave("d", 0, 0, "v")
+            if k == 5:
+                weave("d", 0, 1, "v")
+                quant("d", 0, 0)
+            if k == 6:
+                quant("d", 0, 1)
             turn_out(g, j)
-            if j >= 1:
+            if 1 <= k < 7:
                 out0_mult(k - 1)
                 out0_empty(k - 1, "ss")
 
-        weave_pe("w", 0, 0)
-        weave_pe("w", 0, 1)
-        weave_pe("w", 1, 0)
-        weave_out("w", 0, 0)
-        weave_pe("w", 1, 1)
-        weave_out("w", 0, 1)
+        weave("w", 0, 0, "v")
+        weave("w", 0, 1, "s")
+        weave("w", 1, 0, "v")
+        weave("w", 1, 1, "s")
         quant("w", 0, 0)
-        weave_out("w", 1, 0)
-        quant("w", 0, 1)
-        weave_out("w", 1, 1)
-        square(0, 0)
-        gate(0, 0)
         quant("w", 1, 0)
+        quant("w", 0, 1)
+        weave("r", 0, 0, "v")
+        weave("r", 0, 1, "s")
         quant("w", 1, 1)
-        for k in range(4):
-            step(k, k < 3)
-        weave("d", 0, 0, "v")
-        turn_quant(0, 3)
-        weave_pe("r", 0, 0)
-        weave_pe("r", 0, 1)
-        out0_mult(3)
-        weave("d", 0, 1, "v")
-        quant("d", 0, 0)
-        weave_out("r", 0, 0)
-        weave_out("r", 0, 1)
-        out0_empty(3, "ss")
         weave("r", 1, 0, "v")
-        quant("d", 0, 1)
+        weave("r", 1, 1, "s")
         quant("r", 0, 0)
         quant("r", 0, 1)
-        square(1, 0)
-        gate(1, 0)
+        square(0, 0)
+        gate(0, 0)
         quant("r", 1, 0)
-        weave("r", 1, 1, "s")
-        for k in range(4, 8):
-            step(k, k < 7)
-            if k == 4:
-                quant("r", 1, 1)
+        for k in range(8):
+            step(k)
         weave("d", 1, 0, "v")
+        turn_quant(1, 2)
+        quant("d", 1, 0)
         weave("d", 1, 1, "v")
         turn_quant(1, 3)
-        quant("d", 1, 0)
-        out0_mult(7)
         quant("d", 1, 1)
+        out0_mult(6)
         out1_mult(0)
+        out0_empty(6, "ss")
+        out1_mult(1)
+        out1_empty(0, "sv")
+        out0_mult(7)
+        out1_empty(1, "sv")
+        out1_mult(2)
         out0_empty(7, "sv")
-        for f in range(1, 8):
+        for f in range(3, 8):
             out1_mult(f)
             out1_empty(f - 1, "sv")
         out1_empty(7, "sv")

@@ -127,8 +127,8 @@ def tile_gatedcrossattention_pb_v_kernel(tc, query, hr, Wu, bu, Wh, bh, u, h, gr
 
         def weave(nm, g, n, eng):
             inter = stage.tile([P, NH * J], BF16, name="inter", align_bytes=64)
-            view = rows[(nm, g)][:, :, n * NH:(n + 1) * NH].rearrange("p j w -> p w j")
-            dst = inter[:].rearrange("p (w j) -> p w j", j=J)
+            view = rows[(nm, g)][:, :, n * NH:(n + 1) * NH].rearrange("p j (c i) -> p c j i", i=4)
+            dst = inter[:].rearrange("p (c i j) -> p c j i", i=4, j=J)
             if eng == "s":
                 nc.scalar.copy(out=dst, in_=view)
             else:
@@ -185,10 +185,9 @@ def tile_gatedcrossattention_pb_v_kernel(tc, query, hr, Wu, bu, Wh, bh, u, h, gr
             g, j = k // J, k % J
             dz(g, j)
             turn(g, j)
-            if k < 7:
-                square((k + 1) // J, (k + 1) % J)
-                gate((k + 1) // J, (k + 1) % J)
-            if 1 <= k < 7:
+            square((k + 1) // J, (k + 1) % J)
+            gate((k + 1) // J, (k + 1) % J)
+            if k >= 1:
                 turn_quant((k - 1) // J, (k - 1) % J)
             if k == 0:
                 quant("r", 1, 1)
@@ -200,7 +199,7 @@ def tile_gatedcrossattention_pb_v_kernel(tc, query, hr, Wu, bu, Wh, bh, u, h, gr
             if k == 6:
                 quant("d", 0, 1)
             turn_out(g, j)
-            if 1 <= k < 7:
+            if k >= 1:
                 out0_mult(k - 1)
                 out0_empty(k - 1, "ss")
 
@@ -221,23 +220,26 @@ def tile_gatedcrossattention_pb_v_kernel(tc, query, hr, Wu, bu, Wh, bh, u, h, gr
         square(0, 0)
         gate(0, 0)
         quant("r", 1, 0)
-        for k in range(8):
+        for k in range(7):
             step(k)
-        weave("d", 1, 0, "v")
         turn_quant(1, 2)
-        quant("d", 1, 0)
-        weave("d", 1, 1, "v")
-        turn_quant(1, 3)
-        quant("d", 1, 1)
+        dz(1, 3)
+        turn(1, 3)
         out0_mult(6)
-        out1_mult(0)
+        turn_out(1, 3)
         out0_empty(6, "ss")
-        out1_mult(1)
-        out1_empty(0, "sv")
+        weave("d", 1, 0, "v")
+        turn_quant(1, 3)
+        quant("d", 1, 0)
         out0_mult(7)
-        out1_empty(1, "sv")
+        weave("d", 1, 1, "v")
+        out0_empty(7, "ss")
+        out1_mult(0)
+        out1_mult(1)
+        out1_empty(0, "ss")
+        quant("d", 1, 1)
         out1_mult(2)
-        out0_empty(7, "sv")
+        out1_empty(1, "sv")
         for f in range(3, 8):
             out1_mult(f)
             out1_empty(f - 1, "sv")

@@ -40,7 +40,8 @@ def tile_gatedcrossattention_pb_v_kernel(tc, query, hr, Wu, bu, Wh, bh, u, h, gr
         tstage = ctx.enter_context(tc.tile_pool(name="tstage", bufs=3))
         ostage = ctx.enter_context(tc.tile_pool(name="ostage", bufs=7))
         tpsum = ctx.enter_context(tc.psum_pool(name="tpsum", bufs=2))
-        apsum = ctx.enter_context(tc.psum_pool(name="apsum", bufs=6))
+        apsum = ctx.enter_context(tc.psum_pool(name="apsum", bufs=2))
+        ppsum = ctx.enter_context(tc.psum_pool(name="ppsum", bufs=4))
         ctx.enter_context(tc.manual_schedule())
 
         ident = const.tile([P, P], F32, name="ident")
@@ -87,17 +88,17 @@ def tile_gatedcrossattention_pb_v_kernel(tc, query, hr, Wu, bu, Wh, bh, u, h, gr
 
         live = {}
 
-        def square(g, j):
+        def square(g, j, lo=0, hi=E):
             hs = src[(g, j)][2]
-            nc.scalar.activation(out=hs[:], in_=hs[:], func=ACT.Square)
+            nc.scalar.activation(out=hs[:, lo:hi], in_=hs[:, lo:hi], func=ACT.Square)
 
         def gate(g, j):
             gs, us, hs = src[(g, j)]
             nc.vector.scalar_tensor_tensor(out=us[:], in0=gs[:], scalar=-1.0, in1=us[:], op0=ALU.mult, op1=ALU.mult)
 
-        def dz(g, j):
+        def dz(g, j, lo=0, hi=E):
             gs, us, hs = src[(g, j)]
-            nc.vector.scalar_tensor_tensor(out=rows[("d", g)][:, j, :], in0=hs[:], scalar=1.0, in1=us[:], op0=ALU.subtract, op1=ALU.mult)
+            nc.vector.scalar_tensor_tensor(out=rows[("d", g)][:, j, lo:hi], in0=hs[:, lo:hi], scalar=1.0, in1=us[:, lo:hi], op0=ALU.subtract, op1=ALU.mult)
 
         def turn(g, j):
             words = rows[("d", g)][:, j, :].bitcast(F32)
@@ -143,10 +144,16 @@ def tile_gatedcrossattention_pb_v_kernel(tc, query, hr, Wu, bu, Wh, bh, u, h, gr
                 in_=inter[:],
             )
 
-        def mult(key, lc, ls, rn):
+        def mult(key, lc, ls, rn, pool, passes):
             for n in range(2):
-                acc = apsum.tile([P, NH], F32, name="acc")
-                for c in range(G):
+                if passes[0] == 0:
+                    if pool == "pre":
+                        acc = ppsum.tile([P, NH], F32, name="pre")
+                    else:
+                        acc = apsum.tile([P, NH], F32, name="acc")
+                    live[("acc", key, n)] = acc
+                acc = live[("acc", key, n)]
+                for c in passes:
                     nc.tensor.matmul_mx(
                         out=acc[:],
                         lhsT=lc[c].bitcast(E5),
@@ -156,7 +163,6 @@ def tile_gatedcrossattention_pb_v_kernel(tc, query, hr, Wu, bu, Wh, bh, u, h, gr
                         start=(c == 0),
                         stop=(c == G - 1),
                     )
-                live[("acc", key, n)] = acc
 
         def empty(key, dest, engs):
             o = ostage.tile([P, E], F32, name="o")
@@ -168,15 +174,15 @@ def tile_gatedcrossattention_pb_v_kernel(tc, query, hr, Wu, bu, Wh, bh, u, h, gr
                     nc.vector.tensor_copy(out=o[:, n * NH:(n + 1) * NH], in_=acc[:])
             nc.sync.dma_start(out=dest, in_=o[:])
 
-        def out0_mult(k):
-            mult(("a", k), [t_codes[:, k, c, :] for c in range(G)], [t_scales[:, k, c, :] for c in range(G)], "w")
+        def out0_mult(k, pool="acc"):
+            mult(("a", k), [t_codes[:, k, c, :] for c in range(G)], [t_scales[:, k, c, :] for c in range(G)], "w", pool, (0, 1))
 
         def out0_empty(k, engs):
             empty(("a", k), o0v[:, k // J, k % J, :], engs)
 
-        def out1_mult(f):
+        def out1_mult(f, pool, passes=(0, 1)):
             mult(("b", f), [codes["d"][:, c, f * P:(f + 1) * P] for c in range(G)],
-                 [scales["d"][:, c, f * P:(f + 1) * P] for c in range(G)], "r")
+                 [scales["d"][:, c, f * P:(f + 1) * P] for c in range(G)], "r", pool, passes)
 
         def out1_empty(f, engs):
             empty(("b", f), o1v[:, f, :], engs)
@@ -194,11 +200,11 @@ def tile_gatedcrossattention_pb_v_kernel(tc, query, hr, Wu, bu, Wh, bh, u, h, gr
             if k == 4:
                 weave("d", 0, 0, "v")
             if k == 5:
-                weave("d", 0, 1, "v")
                 quant("d", 0, 0)
-            if k == 6:
-                quant("d", 0, 1)
             turn_out(g, j)
+            if k == 5:
+                square(1, 3, 0, NH)
+                square(1, 3, NH, E)
             if k >= 1:
                 out0_mult(k - 1)
                 out0_empty(k - 1, "ss")
@@ -220,27 +226,47 @@ def tile_gatedcrossattention_pb_v_kernel(tc, query, hr, Wu, bu, Wh, bh, u, h, gr
         square(0, 0)
         gate(0, 0)
         quant("r", 1, 0)
-        for k in range(7):
+        for k in range(6):
             step(k)
-        turn_quant(1, 2)
-        dz(1, 3)
-        turn(1, 3)
-        out0_mult(6)
-        turn_out(1, 3)
-        out0_empty(6, "ss")
+        out1_mult(0, "pre", (0,))
+        out1_mult(1, "pre", (0,))
+        dz(1, 2, 0, NH)
+        gate(1, 3)
+        dz(1, 3, 0, NH)
+        turn_quant(1, 1)
         weave("d", 1, 0, "v")
-        turn_quant(1, 3)
+        dz(1, 2, NH, E)
         quant("d", 1, 0)
-        out0_mult(7)
-        weave("d", 1, 1, "v")
-        out0_empty(7, "ss")
-        out1_mult(0)
-        out1_mult(1)
+        out0_mult(5)
+        turn(1, 2)
+        out0_empty(5, "ss")
+        dz(1, 3, NH, E)
+        weave("d", 0, 1, "v")
+        out1_mult(0, "pre", (1,))
+        out1_mult(1, "pre", (1,))
+        turn(1, 3)
+        turn_out(1, 2)
         out1_empty(0, "ss")
+        weave("d", 1, 1, "v")
+        quant("d", 0, 1)
+        out1_mult(2, "acc")
+        out1_empty(1, "ss")
+        turn_out(1, 3)
+        turn_quant(1, 2)
         quant("d", 1, 1)
-        out1_mult(2)
-        out1_empty(1, "sv")
-        for f in range(3, 8):
-            out1_mult(f)
-            out1_empty(f - 1, "sv")
+        turn_quant(1, 3)
+        out1_mult(3, "pre")
+        out1_empty(2, "ss")
+        out0_mult(6)
+        out1_empty(3, "sv")
+        out0_mult(7, "pre")
+        out0_empty(6, "sv")
+        out1_mult(4, "acc")
+        out0_empty(7, "sv")
+        out1_mult(5, "pre")
+        out1_empty(4, "sv")
+        out1_mult(6, "acc")
+        out1_empty(5, "sv")
+        out1_mult(7, "pre")
+        out1_empty(6, "sv")
         out1_empty(7, "sv")

@@ -40,8 +40,7 @@ def tile_gatedcrossattention_pb_v_kernel(tc, query, hr, Wu, bu, Wh, bh, u, h, gr
         tstage = ctx.enter_context(tc.tile_pool(name="tstage", bufs=3))
         ostage = ctx.enter_context(tc.tile_pool(name="ostage", bufs=7))
         tpsum = ctx.enter_context(tc.psum_pool(name="tpsum", bufs=2))
-        apsum = ctx.enter_context(tc.psum_pool(name="apsum", bufs=2))
-        ppsum = ctx.enter_context(tc.psum_pool(name="ppsum", bufs=4))
+        apsum = ctx.enter_context(tc.psum_pool(name="apsum", bufs=6))
         ctx.enter_context(tc.manual_schedule())
 
         ident = const.tile([P, P], F32, name="ident")
@@ -144,13 +143,10 @@ def tile_gatedcrossattention_pb_v_kernel(tc, query, hr, Wu, bu, Wh, bh, u, h, gr
                 in_=inter[:],
             )
 
-        def mult(key, lc, ls, rn, pool, passes):
+        def mult(key, lc, ls, rn, passes):
             for n in range(2):
                 if passes[0] == 0:
-                    if pool == "pre":
-                        acc = ppsum.tile([P, NH], F32, name="pre")
-                    else:
-                        acc = apsum.tile([P, NH], F32, name="acc")
+                    acc = apsum.tile([P, NH], F32, name="acc")
                     live[("acc", key, n)] = acc
                 acc = live[("acc", key, n)]
                 for c in passes:
@@ -174,15 +170,15 @@ def tile_gatedcrossattention_pb_v_kernel(tc, query, hr, Wu, bu, Wh, bh, u, h, gr
                     nc.vector.tensor_copy(out=o[:, n * NH:(n + 1) * NH], in_=acc[:])
             nc.sync.dma_start(out=dest, in_=o[:])
 
-        def out0_mult(k, pool="acc"):
-            mult(("a", k), [t_codes[:, k, c, :] for c in range(G)], [t_scales[:, k, c, :] for c in range(G)], "w", pool, (0, 1))
+        def out0_mult(k):
+            mult(("a", k), [t_codes[:, k, c, :] for c in range(G)], [t_scales[:, k, c, :] for c in range(G)], "w", (0, 1))
 
         def out0_empty(k, engs):
             empty(("a", k), o0v[:, k // J, k % J, :], engs)
 
-        def out1_mult(f, pool, passes=(0, 1)):
+        def out1_mult(f, passes=(0, 1)):
             mult(("b", f), [codes["d"][:, c, f * P:(f + 1) * P] for c in range(G)],
-                 [scales["d"][:, c, f * P:(f + 1) * P] for c in range(G)], "r", pool, passes)
+                 [scales["d"][:, c, f * P:(f + 1) * P] for c in range(G)], "r", passes)
 
         def out1_empty(f, engs):
             empty(("b", f), o1v[:, f, :], engs)
@@ -205,9 +201,10 @@ def tile_gatedcrossattention_pb_v_kernel(tc, query, hr, Wu, bu, Wh, bh, u, h, gr
             if k == 5:
                 square(1, 3, 0, NH)
                 square(1, 3, NH, E)
+            if k >= 2:
+                out0_empty(k - 2, "ss")
             if k >= 1:
                 out0_mult(k - 1)
-                out0_empty(k - 1, "ss")
 
         weave("w", 0, 0, "v")
         weave("w", 0, 1, "s")
@@ -228,8 +225,8 @@ def tile_gatedcrossattention_pb_v_kernel(tc, query, hr, Wu, bu, Wh, bh, u, h, gr
         quant("r", 1, 0)
         for k in range(6):
             step(k)
-        out1_mult(0, "pre", (0,))
-        out1_mult(1, "pre", (0,))
+        out1_mult(0, (0,))
+        out1_mult(1, (0,))
         dz(1, 2, 0, NH)
         gate(1, 3)
         dz(1, 3, 0, NH)
@@ -237,36 +234,35 @@ def tile_gatedcrossattention_pb_v_kernel(tc, query, hr, Wu, bu, Wh, bh, u, h, gr
         weave("d", 1, 0, "v")
         dz(1, 2, NH, E)
         quant("d", 1, 0)
+        out0_empty(4, "ss")
         out0_mult(5)
         turn(1, 2)
-        out0_empty(5, "ss")
         dz(1, 3, NH, E)
         weave("d", 0, 1, "v")
-        out1_mult(0, "pre", (1,))
-        out1_mult(1, "pre", (1,))
+        out1_mult(0, (1,))
+        out1_mult(1, (1,))
         turn(1, 3)
+        out0_empty(5, "ss")
         turn_out(1, 2)
         out1_empty(0, "ss")
         weave("d", 1, 1, "v")
         quant("d", 0, 1)
-        out1_mult(2, "acc")
+        out1_mult(2)
         out1_empty(1, "ss")
         turn_out(1, 3)
         turn_quant(1, 2)
         quant("d", 1, 1)
         turn_quant(1, 3)
-        out1_mult(3, "pre")
+        out1_mult(3)
         out1_empty(2, "ss")
         out0_mult(6)
         out1_empty(3, "sv")
-        out0_mult(7, "pre")
+        out0_mult(7)
         out0_empty(6, "sv")
-        out1_mult(4, "acc")
-        out0_empty(7, "sv")
-        out1_mult(5, "pre")
-        out1_empty(4, "sv")
-        out1_mult(6, "acc")
-        out1_empty(5, "sv")
-        out1_mult(7, "pre")
-        out1_empty(6, "sv")
+        for f in range(4, 8):
+            out1_mult(f)
+            if f == 4:
+                out0_empty(7, "sv")
+            else:
+                out1_empty(f - 1, "sv")
         out1_empty(7, "sv")

from contextlib import ExitStack

import concourse.mybir as mybir
from concourse.masks import make_identity

F32 = mybir.dt.float32
BF16 = mybir.dt.bfloat16
U32 = mybir.dt.uint32
U8 = mybir.dt.uint8
E4 = mybir.dt.float8_e4m3fn_x4
E5 = mybir.dt.float8_e5m2_x4
ALU = mybir.AluOpType
ACT = mybir.ActivationFunctionType

P = 128
E = 1024
G = 2
J = 4
NH = 512

FLOPS = 2 * 2 * 1024 * 1024 * 1024
BYTES = 22 * 1024 * 1024


def tile_gatedcrossattention_pb_v_kernel(tc, query, hr, Wu, bu, Wh, bh, u, h, grad_out, out_0, out_1):
    nc = tc.nc
    gv = grad_out.flatten_outer_dims().rearrange("(g p j) e -> p g j e", g=G, j=J)
    uv = u.flatten_outer_dims().rearrange("(g p j) e -> p g j e", g=G, j=J)
    hv = h.flatten_outer_dims().rearrange("(g p j) e -> p g j e", g=G, j=J)
    rv = hr.flatten_outer_dims().rearrange("(g p j) e -> p g j e", g=G, j=J)
    wv = Wh.rearrange("(g p j) e -> p g j e", g=G, j=J)
    o0v = out_0.flatten_outer_dims().rearrange("(g p j) e -> p g j e", g=G, j=J)
    o1v = out_1.rearrange("(f p) e -> p f e", p=P)

    with ExitStack() as ctx:
        const = ctx.enter_context(tc.tile_pool(name="const", bufs=1))
        raw = ctx.enter_context(tc.tile_pool(name="raw", bufs=1))
        keep = ctx.enter_context(tc.tile_pool(name="keep", bufs=1))
        stage = ctx.enter_context(tc.tile_pool(name="stage", bufs=6))
        tstage = ctx.enter_context(tc.tile_pool(name="tstage", bufs=3))
        ostage = ctx.enter_context(tc.tile_pool(name="ostage", bufs=7))
        tpsum = ctx.enter_context(tc.psum_pool(name="tpsum", bufs=2))
        apsum = ctx.enter_context(tc.psum_pool(name="apsum", bufs=6))
        ctx.enter_context(tc.manual_schedule())

        ident = const.tile([P, P], F32, name="ident")
        make_identity(nc, ident[:])
        warm = const.tile([P, 1], F32, name="warm")
        nc.vector.memset(warm[:], 0.0)
        nc.scalar.activation(out=warm[:], in_=warm[:], func=ACT.Square)

        src = {}
        rows = {}

        def load_tokens(g, j):
            gt = raw.tile([P, E], BF16, name="g%d%d" % (g, j))
            ut = raw.tile([P, E], F32, name="u%d%d" % (g, j))
            ht = raw.tile([P, E], F32, name="h%d%d" % (g, j))
            nc.sync.dma_start(out=gt[:], in_=gv[:, g, j, :])
            nc.sync.dma_start(out=ut[:], in_=uv[:, g, j, :])
            nc.sync.dma_start(out=ht[:], in_=hv[:, g, j, :])
            src[(g, j)] = (gt, ut, ht)

        def load_rows(nm, view, g):
            t = raw.tile([P, J, E], BF16, name="%s%d" % (nm, g))
            nc.sync.dma_start(out=t[:], in_=view[:, g, :, :])
            rows[(nm, g)] = t

        load_rows("w", wv, 0)
        load_rows("w", wv, 1)
        load_rows("r", rv, 0)
        load_rows("r", rv, 1)
        for g in range(G):
            for j in range(J):
                load_tokens(g, j)

        for g in range(G):
            rows[("d", g)] = keep.tile([P, J, E], BF16, name="dz%d" % g)
        codes = {}
        scales = {}
        for nm in ("w", "r", "d"):
            codes[nm] = keep.tile([P, G, E], U32, name="%s_codes" % nm, align_bytes=64)
            scales[nm] = keep.tile([P, G, E], U8, name="%s_scales" % nm, align_bytes=64)
        fmt = {"w": E4, "r": E4, "d": E5}
        t_codes = keep.tile([P, G * J, G, P], U32, name="t_codes", align_bytes=64)
        t_scales = keep.tile([P, G * J, G, P], U8, name="t_scales", align_bytes=64)

        live = {}

        def square(g, j, lo=0, hi=E):
            hs = src[(g, j)][2]
            nc.scalar.activation(out=hs[:, lo:hi], in_=hs[:, lo:hi], func=ACT.Square)

        def gate(g, j):
            gs, us, hs = src[(g, j)]
            nc.vector.scalar_tensor_tensor(out=us[:], in0=gs[:], scalar=-1.0, in1=us[:], op0=ALU.mult, op1=ALU.mult)

        def dz(g, j, lo=0, hi=E):
            gs, us, hs = src[(g, j)]
            nc.vector.scalar_tensor_tensor(out=rows[("d", g)][:, j, lo:hi], in0=hs[:, lo:hi], scalar=1.0, in1=us[:, lo:hi], op0=ALU.subtract, op1=ALU.mult)

        def turn(g, j):
            words = rows[("d", g)][:, j, :].bitcast(F32)
            tp = tpsum.tile([P, 4 * P], F32, name="tp")
            for c in range(G):
                for w in range(2):
                    nc.tensor.transpose(tp[:, (2 * c + w) * P:(2 * c + w + 1) * P], words[:, 256 * c + w:256 * (c + 1):2], ident[:])
            live[("tp", g, j)] = tp

        def turn_out(g, j):
            tp = live.pop(("tp", g, j))
            grouped = tstage.tile([P, 4 * 2 * P], BF16, name="grouped", align_bytes=64)
            nc.scalar.copy(
                out=grouped[:].bitcast(F32).rearrange("p (c m w) -> p c m w", c=G, w=2),
                in_=tp[:].rearrange("p (c w m) -> p c m w", c=G, w=2),
            )
            live[("gr", g, j)] = grouped

        def turn_quant(g, j):
            k = g * J + j
            grouped = live.pop(("gr", g, j))
            nc.vector.quantize_mx(
                out=t_codes[:, k, :, :].rearrange("p c m -> p (c m)").bitcast(E5),
                scales=t_scales[:, k, :, :].rearrange("p c m -> p (c m)"),
                in_=grouped[:],
            )

        def weave(nm, g, n, eng):
            inter = stage.tile([P, NH * J], BF16, name="inter", align_bytes=64)
            view = rows[(nm, g)][:, :, n * NH:(n + 1) * NH].rearrange("p j (c i) -> p c j i", i=4)
            dst = inter[:].rearrange("p (c i j) -> p c j i", i=4, j=J)
            if eng == "s":
                nc.scalar.copy(out=dst, in_=view)
            else:
                nc.vector.tensor_copy(out=dst, in_=view)
            live[("in", nm, g, n)] = inter

        def quant(nm, g, n):
            inter = live.pop(("in", nm, g, n))
            nc.vector.quantize_mx(
                out=codes[nm][:, g, n * NH:(n + 1) * NH].bitcast(fmt[nm]),
                scales=scales[nm][:, g, n * NH:(n + 1) * NH],
                in_=inter[:],
            )

        def mult(key, lc, ls, rn, passes):
            for n in range(2):
                if passes[0] == 0:
                    acc = apsum.tile([P, NH], F32, name="acc")
                    live[("acc", key, n)] = acc
                acc = live[("acc", key, n)]
                for c in passes:
                    nc.tensor.matmul_mx(
                        out=acc[:],
                        lhsT=lc[c].bitcast(E5),
                        lhsT_scale=ls[c],
                        rhs=codes[rn][:, c, n * NH:(n + 1) * NH].bitcast(E4),
                        rhs_scale=scales[rn][:, c, n * NH:(n + 1) * NH],
                        start=(c == 0),
                        stop=(c == G - 1),
                    )

        def empty(key, dest, engs):
            o = ostage.tile([P, E], F32, name="o")
            for n in range(2):
                acc = live.pop(("acc", key, n))
                if engs[n] == "s":
                    nc.scalar.copy(out=o[:, n * NH:(n + 1) * NH], in_=acc[:])
                else:
                    nc.vector.tensor_copy(out=o[:, n * NH:(n + 1) * NH], in_=acc[:])
            nc.sync.dma_start(out=dest, in_=o[:])

        def out0_mult(k):
            mult(("a", k), [t_codes[:, k, c, :] for c in range(G)], [t_scales[:, k, c, :] for c in range(G)], "w", (0, 1))

        def out0_empty(k, engs):
            empty(("a", k), o0v[:, k // J, k % J, :], engs)

        def out1_mult(f, passes=(0, 1)):
            mult(("b", f), [codes["d"][:, c, f * P:(f + 1) * P] for c in range(G)],
                 [scales["d"][:, c, f * P:(f + 1) * P] for c in range(G)], "r", passes)

        def out1_empty(f, engs):
            empty(("b", f), o1v[:, f, :], engs)

        def step(k):
            g, j = k // J, k % J
            dz(g, j)
            turn(g, j)
            square((k + 1) // J, (k + 1) % J)
            gate((k + 1) // J, (k + 1) % J)
            if k >= 1:
                turn_quant((k - 1) // J, (k - 1) % J)
            if k == 0:
                quant("r", 1, 1)
            if k == 4:
                weave("d", 0, 0, "v")
            if k == 5:
                quant("d", 0, 0)
            turn_out(g, j)
            if k == 5:
                square(1, 3, 0, NH)
                square(1, 3, NH, E)
            if k >= 2:
                out0_empty(k - 2, "ss")
            if k >= 1:
                out0_mult(k - 1)

        weave("w", 0, 0, "v")
        weave("w", 0, 1, "s")
        weave("w", 1, 0, "v")
        weave("w", 1, 1, "s")
        quant("w", 0, 0)
        quant("w", 1, 0)
        quant("w", 0, 1)
        weave("r", 0, 0, "v")
        weave("r", 0, 1, "s")
        quant("w", 1, 1)
        weave("r", 1, 0, "v")
        weave("r", 1, 1, "s")
        quant("r", 0, 0)
        quant("r", 0, 1)
        square(0, 0)
        gate(0, 0)
        quant("r", 1, 0)
        for k in range(6):
            step(k)
        out1_mult(0, (0,))
        out1_mult(1, (0,))
        dz(1, 2, 0, NH)
        gate(1, 3)
        dz(1, 3, 0, NH)
        turn_quant(1, 1)
        weave("d", 1, 0, "v")
        dz(1, 2, NH, E)
        quant("d", 1, 0)
        out0_empty(4, "ss")
        out0_mult(5)
        turn(1, 2)
        dz(1, 3, NH, E)
        weave("d", 0, 1, "v")
        out1_mult(0, (1,))
        out1_mult(1, (1,))
        turn(1, 3)
        out0_empty(5, "ss")
        turn_out(1, 2)
        out1_empty(0, "ss")
        weave("d", 1, 1, "v")
        quant("d", 0, 1)
        out1_mult(2)
        out1_empty(1, "ss")
        turn_out(1, 3)
        turn_quant(1, 2)
        quant("d", 1, 1)
        turn_quant(1, 3)
        out1_mult(3)
        out1_empty(2, "ss")
        out0_mult(6)
        out1_empty(3, "sv")
        out0_mult(7)
        out0_empty(6, "sv")
        for f in range(4, 8):
            out1_mult(f)
            if f == 4:
                out0_empty(7, "sv")
            else:
                out1_empty(f - 1, "sv")
        out1_empty(7, "sv")
